import numpy as np
import ml_dtypes


def mxq(x, axis, fmt="e4m3"):
    dtype, down = {"e4m3": (ml_dtypes.float8_e4m3fn, 7), "e5m2": (ml_dtypes.float8_e5m2, 14)}[fmt]
    v = np.moveaxis(np.asarray(x, np.float32).astype(ml_dtypes.bfloat16).astype(np.float64), axis, -1)
    blocks = v.reshape(v.shape[:-1] + (-1, 32))
    amax = np.abs(blocks).max(-1, keepdims=True)
    byte = np.maximum(np.where(amax > 0, np.frexp(amax)[1] - 1 + 127, 0) - down, 1)
    scale = np.exp2(byte - 127.0)
    codes = (blocks / scale).astype(np.float32).astype(dtype).astype(np.float64)
    return np.moveaxis((codes * scale).reshape(v.shape), -1, axis)


WIDE = False


def mx_kscale(k):
    if not WIDE:
        return np.ones(k)
    levels = np.array([10, -10, 5, -5, 0])
    a = np.random.permutation(np.resize(levels, k // 512 * 4)).reshape(k // 512, 4)
    idx = np.arange(k)
    return np.exp2(a[idx // 512, idx % 128 // 32])


BF16 = ml_dtypes.bfloat16


def bf(x):
    return np.asarray(x, np.float32).astype(BF16)


def f64(x):
    return np.asarray(x).astype(np.float64)


B, IN, H = 512, 512, 1024


def sigmoid(v):
    return 1.0 / (1.0 + np.exp(-v))


def setup_inputs():
    s = mx_kscale(IN)
    g = np.random.standard_normal((H, IN + H)) / np.sqrt(IN + H)
    g[:, :IN] /= s
    return {"x": bf(np.random.standard_normal((B, IN)) * s),
            "h": bf(np.random.standard_normal((B, H))),
            "tau": bf(np.random.standard_normal(H)),
            "W_in": bf(np.random.standard_normal((H, IN)) / np.sqrt(IN) / s),
            "W_rec": bf(np.random.standard_normal((H, H)) * 1.5 / np.sqrt(H)),
            "gate_w": bf(g),
            "gate_b": bf(np.random.standard_normal(H) * 0.5)}


def reference(x, h, tau, W_in, W_rec, gate_w, gate_b):
    tau_p = np.log(1.0 + np.exp(f64(tau))) + 1.0
    g = f64(gate_w)
    xq = mxq(f64(x), 1, "e4m3")
    hq = mxq(f64(h), 1, "e4m3")
    x_in = xq @ mxq(f64(W_in), 1, "e4m3").T
    pre = (xq @ mxq(g[:, :IN], 1, "e4m3").T) + (hq @ mxq(g[:, IN:], 1, "e4m3").T) + f64(gate_b)
    gate = sigmoid(np.tanh(pre))
    k1 = -f64(h) / tau_p + x_in + gate * (hq @ mxq(f64(W_rec), 1, "e4m3").T)
    return x_in, k1

@@ -1,0 +1,205 @@
+from contextlib import ExitStack
+
+import concourse.mybir as mybir
+from concourse.masks import make_identity
+
+F32 = mybir.dt.float32
+BF16 = mybir.dt.bfloat16
+U32 = mybir.dt.uint32
+U8 = mybir.dt.uint8
+FP8X4 = mybir.dt.float8_e4m3fn_x4
+ACT = mybir.ActivationFunctionType
+ALU = mybir.AluOpType
+
+P = 128
+B, IN, H = 512, 512, 1024
+OB = 256
+NBLK = H // OB
+FLOPS = 2 * B * H * (IN + IN + H + H)
+
+ACT_COPY = ["v", "v", "v", "v", "v", "v"]
+W_COPY = ["s", "s", "s", "s", "s", "s"]
+
+
+def tile_ltccell_pa_kernel(tc, x, h, tau, W_in, W_rec, gate_w, gate_b, out_0, out_1):
+    nc = tc.nc
+    with ExitStack() as ctx:
+        keep = ctx.enter_context(tc.tile_pool(name="keep", bufs=1))
+        stage = ctx.enter_context(tc.tile_pool(name="stage", bufs=4))
+        work = ctx.enter_context(tc.tile_pool(name="work", bufs=3))
+        ps_t = ctx.enter_context(tc.psum_pool(name="ps_t", bufs=3))
+        ps_a = ctx.enter_context(tc.psum_pool(name="ps_a", bufs=2))
+        ps_x = ctx.enter_context(tc.psum_pool(name="ps_x", bufs=1))
+
+        ident = keep.tile([P, P], F32, name="ident")
+        make_identity(nc, ident[:])
+
+        tg = keep.tile([P, 2 * P], BF16, name="tg")
+        nc.vector.memset(tg[:], 0.0)
+        nc.sync.dma_start(out=tg[0:8, 0:P], in_=tau.rearrange("(r c) -> r c", c=P))
+        nc.sync.dma_start(out=tg[0:8, P:2 * P], in_=gate_b.rearrange("(r c) -> r c", c=P))
+
+        x_v = x.rearrange("(i p) k -> p i k", p=P)
+        h_v = h.rearrange("(i p) k -> p i k", p=P)
+        x_sb, h_sb = [], []
+        for bp in range(2):
+            xt = keep.tile([P, 2 * IN], BF16, name="x_sb%d" % bp)
+            nc.sync.dma_start(out=xt[:].rearrange("p (i k) -> p i k", i=2), in_=x_v[:, 2 * bp:2 * bp + 2, :])
+            x_sb.append(xt)
+        for bp in range(2):
+            ht = keep.tile([P, 2 * H], BF16, name="h_sb%d" % bp)
+            nc.sync.dma_start(out=ht[:].rearrange("p (i k) -> p i k", i=2), in_=h_v[:, 2 * bp:2 * bp + 2, :])
+            h_sb.append(ht)
+
+        g_v = gate_w.rearrange("(t p) k -> p t k", p=P)
+        r_v = W_rec.rearrange("(t p) k -> p t k", p=P)
+        i_v = W_in.rearrange("(t p) k -> p t k", p=P)
+        gw_sb, wr_sb, wi_sb = [], [], []
+        for j in range(NBLK):
+            gt = keep.tile([P, 2 * (IN + H)], BF16, name="gw_sb%d" % j)
+            nc.sync.dma_start(out=gt[:].rearrange("p (t k) -> p t k", t=2), in_=g_v[:, 2 * j:2 * j + 2, :])
+            rt = keep.tile([P, 2 * H], BF16, name="wr_sb%d" % j)
+            nc.sync.dma_start(out=rt[:].rearrange("p (t k) -> p t k", t=2), in_=r_v[:, 2 * j:2 * j + 2, :])
+            it = keep.tile([P, 2 * IN], BF16, name="wi_sb%d" % j)
+            nc.sync.dma_start(out=it[:].rearrange("p (t k) -> p t k", t=2), in_=i_v[:, 2 * j:2 * j + 2, :])
+            gw_sb.append(gt)
+            wr_sb.append(rt)
+            wi_sb.append(it)
+
+        def flip_pair(sources, engines, codes, scales):
+            grouped = stage.tile([P, 2048], BF16, name="grouped", align_bytes=64)
+            g32 = grouped[:].bitcast(F32)
+            for half in range(2):
+                src, row_words, first = sources[half]
+                s32 = src[:].bitcast(F32)
+                bank = ps_t.tile([P, 2, 2 * P], F32, name="bank")
+                for t in range(2):
+                    for u in range(2):
+                        c0 = t * row_words + first + u * P
+                        nc.tensor.transpose(bank[:, u, t * P:(t + 1) * P], s32[:, c0:c0 + P], ident[:])
+                dst = g32[:, half * 512:(half + 1) * 512].rearrange("p (r u) -> p r u", u=2)
+                if engines[half] == "v":
+                    nc.vector.tensor_copy(out=dst, in_=bank[:].rearrange("p u r -> p r u"))
+                else:
+                    nc.scalar.copy(out=dst, in_=bank[:].rearrange("p u r -> p r u"))
+            nc.vector.quantize_mx(out=codes.bitcast(FP8X4), scales=scales, in_=grouped[:])
+
+        xq = keep.tile([P, 512], U32, name="xq", align_bytes=64)
+        xs = keep.tile([P, 512], U8, name="xs", align_bytes=64)
+        hq = keep.tile([P, 1024], U32, name="hq", align_bytes=64)
+        hs = keep.tile([P, 1024], U8, name="hs", align_bytes=64)
+        flip_pair([(x_sb[0], IN // 2, 0), (x_sb[1], IN // 2, 0)], ACT_COPY[0:2], xq[:], xs[:])
+        for bp in range(2):
+            flip_pair([(h_sb[bp], H // 2, 0), (h_sb[bp], H // 2, 256)], ACT_COPY[2 + 2 * bp:4 + 2 * bp],
+                      hq[:, bp * 512:(bp + 1) * 512], hs[:, bp * 512:(bp + 1) * 512])
+
+        ab = keep.tile([P, P], F32, name="ab")
+        nc.scalar.activation(out=ab[:], in_=tg[:, 0:P], func=ACT.Abs)
+        ex = keep.tile([P, P], F32, name="ex")
+        nc.scalar.activation(out=ex[:], in_=ab[:], func=ACT.Exp, scale=-1.0)
+        e1 = keep.tile([P, P], F32, name="e1")
+        nc.vector.tensor_scalar_add(out=e1[:], in0=ex[:], scalar1=1.0)
+        ln = keep.tile([P, P], F32, name="ln")
+        nc.scalar.activation(out=ln[:], in_=e1[:], func=ACT.Ln)
+        rl = keep.tile([P, P], F32, name="rl")
+        nc.vector.tensor_scalar_max(out=rl[:], in0=tg[:, 0:P], scalar1=0.0)
+        tp = keep.tile([P, P], F32, name="tp")
+        nc.vector.scalar_tensor_tensor(out=tp[:], in0=ln[:], scalar=1.0, in1=rl[:], op0=ALU.add, op1=ALU.add)
+        rc = keep.tile([P, P], F32, name="rc")
+        nc.vector.reciprocal(out=rc[:], in_=tp[:])
+        gb = keep.tile([P, P], F32, name="gb")
+        nc.vector.tensor_copy(out=gb[:], in_=tg[:, P:2 * P])
+
+        rc_bc = keep.tile([P, H], F32, name="rc_bc")
+        gb_bc = keep.tile([P, H], F32, name="gb_bc")
+        for half in range(2):
+            pr = ps_a.tile([P, 512], F32, name="pre")
+            pg = ps_a.tile([P, 512], F32, name="rec")
+            for q in range(4):
+                r = half * 4 + q
+                sel = ident[:, r:r + 1].to_broadcast([P, P])
+                nc.tensor.matmul(out=pr[:, q * P:(q + 1) * P], lhsT=sel, rhs=rc[:], start=True, stop=True)
+            for q in range(4):
+                r = half * 4 + q
+                sel = ident[:, r:r + 1].to_broadcast([P, P])
+                nc.tensor.matmul(out=pg[:, q * P:(q + 1) * P], lhsT=sel, rhs=gb[:], start=True, stop=True)
+            nc.vector.tensor_copy(out=rc_bc[:, half * 512:(half + 1) * 512], in_=pr[:])
+            nc.scalar.copy(out=gb_bc[:, half * 512:(half + 1) * 512], in_=pg[:])
+
+        leak = []
+        for bp in range(2):
+            lk = keep.tile([P, 2 * H], F32, name="leak%d" % bp)
+            for s in range(2):
+                nc.vector.tensor_tensor(out=lk[:, s * H:(s + 1) * H], in0=h_sb[bp][:, s * H:(s + 1) * H],
+                                        in1=rc_bc[:], op=ALU.mult)
+            leak.append(lk)
+
+        wq, ws = [], []
+
+        def flip_block(j):
+            cq = keep.tile([P, 6 * OB], U32, name="wq%d" % j, align_bytes=64)
+            cs = keep.tile([P, 6 * OB], U8, name="ws%d" % j, align_bytes=64)
+            gwords = (IN + H) // 2
+            srcs = [(gw_sb[j], gwords, 0), (gw_sb[j], gwords, 256), (gw_sb[j], gwords, 512),
+                    (wr_sb[j], H // 2, 0), (wr_sb[j], H // 2, 256), (wi_sb[j], IN // 2, 0)]
+            for pair in range(3):
+                flip_pair(srcs[2 * pair:2 * pair + 2], W_COPY[2 * pair:2 * pair + 2],
+                          cq[:, pair * 512:(pair + 1) * 512], cs[:, pair * 512:(pair + 1) * 512])
+            wq.append(cq)
+            ws.append(cs)
+
+        o0_v = out_0.rearrange("(i p) o -> p i o", p=P)
+        o1_v = out_1.rearrange("(i p) o -> p i o", p=P)
+
+        def mx(out, a_codes, a_scales, a0, j, q, start, stop):
+            nc.tensor.matmul_mx(out=out,
+                                lhsT=a_codes[:, a0:a0 + P].bitcast(FP8X4), lhsT_scale=a_scales[:, a0:a0 + P],
+                                rhs=wq[j][:, q * OB:(q + 1) * OB].bitcast(FP8X4),
+                                rhs_scale=ws[j][:, q * OB:(q + 1) * OB],
+                                start=start, stop=stop)
+
+        def round_(j, bp):
+            pre = ps_a.tile([P, 512], F32, name="pre")
+            rec = ps_a.tile([P, 512], F32, name="rec")
+            xin = ps_x.tile([P, 512], F32, name="xin")
+            for s in range(2):
+                o = pre[:, s * OB:(s + 1) * OB]
+                mx(o, xq, xs, bp * 256 + s * P, j, 0, True, False)
+                mx(o, hq, hs, bp * 512 + s * P, j, 1, False, False)
+                mx(o, hq, hs, bp * 512 + 256 + s * P, j, 2, False, True)
+            for s in range(2):
+                o = rec[:, s * OB:(s + 1) * OB]
+                mx(o, hq, hs, bp * 512 + s * P, j, 3, True, False)
+                mx(o, hq, hs, bp * 512 + 256 + s * P, j, 4, False, True)
+            for s in range(2):
+                mx(xin[:, s * OB:(s + 1) * OB], xq, xs, bp * 256 + s * P, j, 5, True, True)
+
+            cols = slice(j * OB, (j + 1) * OB)
+            xin_sb = work.tile([P, 512], F32, name="xin_sb")
+            nc.scalar.copy(out=xin_sb[:], in_=xin[:])
+            nc.sync.dma_start(out=o0_v[:, 2 * bp:2 * bp + 2, cols], in_=xin_sb[:].rearrange("p (s n) -> p s n", s=2))
+
+            u = work.tile([P, 512], F32, name="u")
+            nc.vector.tensor_tensor(out=u[:].rearrange("p (s n) -> p s n", s=2),
+                                    in0=pre[:].rearrange("p (s n) -> p s n", s=2),
+                                    in1=gb_bc[:, cols].unsqueeze(1).to_broadcast([P, 2, OB]), op=ALU.add)
+            t1 = work.tile([P, 512], F32, name="t1")
+            nc.scalar.activation(out=t1[:], in_=u[:], func=ACT.Tanh)
+            t2 = work.tile([P, 512], F32, name="t2")
+            nc.scalar.activation(out=t2[:], in_=t1[:], func=ACT.Tanh, scale=0.5)
+            m2 = work.tile([P, 512], F32, name="m2")
+            nc.vector.tensor_tensor(out=m2[:].rearrange("p (s n) -> p s n", s=2),
+                                    in0=xin_sb[:].rearrange("p (s n) -> p s n", s=2),
+                                    in1=leak[bp][:].rearrange("p (s o) -> p s o", s=2)[:, :, cols], op=ALU.subtract)
+            w = work.tile([P, 512], F32, name="w")
+            nc.vector.scalar_tensor_tensor(out=w[:], in0=t2[:], scalar=1.0, in1=rec[:], op0=ALU.add, op1=ALU.mult)
+            k1 = work.tile([P, 512], F32, name="k1")
+            nc.vector.scalar_tensor_tensor(out=k1[:], in0=w[:], scalar=0.5, in1=m2[:], op0=ALU.mult, op1=ALU.add)
+            nc.sync.dma_start(out=o1_v[:, 2 * bp:2 * bp + 2, cols], in_=k1[:].rearrange("p (s n) -> p s n", s=2))
+
+        flip_block(0)
+        for j in range(NBLK):
+            if j + 1 < NBLK:
+                flip_block(j + 1)
+            round_(j, 0)
+            round_(j, 1)

@@ -15,10 +15,16 @@ P = 128
 B, IN, H = 512, 512, 1024
 OB = 256
 NBLK = H // OB
+NROUND = 2 * NBLK
 FLOPS = 2 * B * H * (IN + IN + H + H)
 
-ACT_COPY = ["v", "v", "v", "v", "v", "v"]
-W_COPY = ["s", "s", "s", "s", "s", "s"]
+PIN = True
+LEAK_ENG = "g"
+G_ENG = "g"
+LEAD = 2
+LEAD_ENG = "ss"
+VCP = "vvvvvvvv"
+W0 = "vsvsvs"
 
 
 def tile_ltccell_pa_kernel(tc, x, h, tau, W_in, W_rec, gate_w, gate_b, out_0, out_1):
@@ -26,13 +32,18 @@ def tile_ltccell_pa_kernel(tc, x, h, tau, W_in, W_rec, gate_w, gate_b, out_0, ou
     with ExitStack() as ctx:
         keep = ctx.enter_context(tc.tile_pool(name="keep", bufs=1))
         stage = ctx.enter_context(tc.tile_pool(name="stage", bufs=4))
-        work = ctx.enter_context(tc.tile_pool(name="work", bufs=3))
+        work = ctx.enter_context(tc.tile_pool(name="work", bufs=4))
         ps_t = ctx.enter_context(tc.psum_pool(name="ps_t", bufs=3))
-        ps_a = ctx.enter_context(tc.psum_pool(name="ps_a", bufs=2))
+        ps_p = ctx.enter_context(tc.psum_pool(name="ps_p", bufs=2))
+        ps_r = ctx.enter_context(tc.psum_pool(name="ps_r", bufs=2))
         ps_x = ctx.enter_context(tc.psum_pool(name="ps_x", bufs=1))
+        if PIN:
+            ctx.enter_context(tc.manual_schedule())
 
         ident = keep.tile([P, P], F32, name="ident")
         make_identity(nc, ident[:])
+        identb = keep.tile([P, P], BF16, name="identb")
+        make_identity(nc, identb[:])
 
         tg = keep.tile([P, 2 * P], BF16, name="tg")
         nc.vector.memset(tg[:], 0.0)
@@ -58,148 +69,285 @@ def tile_ltccell_pa_kernel(tc, x, h, tau, W_in, W_rec, gate_w, gate_b, out_0, ou
         for j in range(NBLK):
             gt = keep.tile([P, 2 * (IN + H)], BF16, name="gw_sb%d" % j)
             nc.sync.dma_start(out=gt[:].rearrange("p (t k) -> p t k", t=2), in_=g_v[:, 2 * j:2 * j + 2, :])
-            rt = keep.tile([P, 2 * H], BF16, name="wr_sb%d" % j)
-            nc.sync.dma_start(out=rt[:].rearrange("p (t k) -> p t k", t=2), in_=r_v[:, 2 * j:2 * j + 2, :])
             it = keep.tile([P, 2 * IN], BF16, name="wi_sb%d" % j)
             nc.sync.dma_start(out=it[:].rearrange("p (t k) -> p t k", t=2), in_=i_v[:, 2 * j:2 * j + 2, :])
+            rt = keep.tile([P, 2 * H], BF16, name="wr_sb%d" % j)
+            nc.sync.dma_start(out=rt[:].rearrange("p (t k) -> p t k", t=2), in_=r_v[:, 2 * j:2 * j + 2, :])
             gw_sb.append(gt)
             wr_sb.append(rt)
             wi_sb.append(it)
-
-        def flip_pair(sources, engines, codes, scales):
-            grouped = stage.tile([P, 2048], BF16, name="grouped", align_bytes=64)
-            g32 = grouped[:].bitcast(F32)
-            for half in range(2):
-                src, row_words, first = sources[half]
-                s32 = src[:].bitcast(F32)
-                bank = ps_t.tile([P, 2, 2 * P], F32, name="bank")
-                for t in range(2):
-                    for u in range(2):
-                        c0 = t * row_words + first + u * P
-                        nc.tensor.transpose(bank[:, u, t * P:(t + 1) * P], s32[:, c0:c0 + P], ident[:])
-                dst = g32[:, half * 512:(half + 1) * 512].rearrange("p (r u) -> p r u", u=2)
-                if engines[half] == "v":
-                    nc.vector.tensor_copy(out=dst, in_=bank[:].rearrange("p u r -> p r u"))
-                else:
-                    nc.scalar.copy(out=dst, in_=bank[:].rearrange("p u r -> p r u"))
-            nc.vector.quantize_mx(out=codes.bitcast(FP8X4), scales=scales, in_=grouped[:])
 
         xq = keep.tile([P, 512], U32, name="xq", align_bytes=64)
         xs = keep.tile([P, 512], U8, name="xs", align_bytes=64)
         hq = keep.tile([P, 1024], U32, name="hq", align_bytes=64)
         hs = keep.tile([P, 1024], U8, name="hs", align_bytes=64)
-        flip_pair([(x_sb[0], IN // 2, 0), (x_sb[1], IN // 2, 0)], ACT_COPY[0:2], xq[:], xs[:])
-        for bp in range(2):
-            flip_pair([(h_sb[bp], H // 2, 0), (h_sb[bp], H // 2, 256)], ACT_COPY[2 + 2 * bp:4 + 2 * bp],
-                      hq[:, bp * 512:(bp + 1) * 512], hs[:, bp * 512:(bp + 1) * 512])
-
-        ab = keep.tile([P, P], F32, name="ab")
-        nc.scalar.activation(out=ab[:], in_=tg[:, 0:P], func=ACT.Abs)
-        ex = keep.tile([P, P], F32, name="ex")
-        nc.scalar.activation(out=ex[:], in_=ab[:], func=ACT.Exp, scale=-1.0)
-        e1 = keep.tile([P, P], F32, name="e1")
-        nc.vector.tensor_scalar_add(out=e1[:], in0=ex[:], scalar1=1.0)
-        ln = keep.tile([P, P], F32, name="ln")
-        nc.scalar.activation(out=ln[:], in_=e1[:], func=ACT.Ln)
-        rl = keep.tile([P, P], F32, name="rl")
-        nc.vector.tensor_scalar_max(out=rl[:], in0=tg[:, 0:P], scalar1=0.0)
-        tp = keep.tile([P, P], F32, name="tp")
-        nc.vector.scalar_tensor_tensor(out=tp[:], in0=ln[:], scalar=1.0, in1=rl[:], op0=ALU.add, op1=ALU.add)
-        rc = keep.tile([P, P], F32, name="rc")
-        nc.vector.reciprocal(out=rc[:], in_=tp[:])
-        gb = keep.tile([P, P], F32, name="gb")
-        nc.vector.tensor_copy(out=gb[:], in_=tg[:, P:2 * P])
-
-        rc_bc = keep.tile([P, H], F32, name="rc_bc")
-        gb_bc = keep.tile([P, H], F32, name="gb_bc")
-        for half in range(2):
-            pr = ps_a.tile([P, 512], F32, name="pre")
-            pg = ps_a.tile([P, 512], F32, name="rec")
-            for q in range(4):
-                r = half * 4 + q
-                sel = ident[:, r:r + 1].to_broadcast([P, P])
-                nc.tensor.matmul(out=pr[:, q * P:(q + 1) * P], lhsT=sel, rhs=rc[:], start=True, stop=True)
-            for q in range(4):
-                r = half * 4 + q
-                sel = ident[:, r:r + 1].to_broadcast([P, P])
-                nc.tensor.matmul(out=pg[:, q * P:(q + 1) * P], lhsT=sel, rhs=gb[:], start=True, stop=True)
-            nc.vector.tensor_copy(out=rc_bc[:, half * 512:(half + 1) * 512], in_=pr[:])
-            nc.scalar.copy(out=gb_bc[:, half * 512:(half + 1) * 512], in_=pg[:])
-
-        leak = []
-        for bp in range(2):
-            lk = keep.tile([P, 2 * H], F32, name="leak%d" % bp)
-            for s in range(2):
-                nc.vector.tensor_tensor(out=lk[:, s * H:(s + 1) * H], in0=h_sb[bp][:, s * H:(s + 1) * H],
-                                        in1=rc_bc[:], op=ALU.mult)
-            leak.append(lk)
-
         wq, ws = [], []
-
-        def flip_block(j):
+        for j in range(NBLK):
             cq = keep.tile([P, 6 * OB], U32, name="wq%d" % j, align_bytes=64)
             cs = keep.tile([P, 6 * OB], U8, name="ws%d" % j, align_bytes=64)
-            gwords = (IN + H) // 2
-            srcs = [(gw_sb[j], gwords, 0), (gw_sb[j], gwords, 256), (gw_sb[j], gwords, 512),
-                    (wr_sb[j], H // 2, 0), (wr_sb[j], H // 2, 256), (wi_sb[j], IN // 2, 0)]
-            for pair in range(3):
-                flip_pair(srcs[2 * pair:2 * pair + 2], W_COPY[2 * pair:2 * pair + 2],
-                          cq[:, pair * 512:(pair + 1) * 512], cs[:, pair * 512:(pair + 1) * 512])
             wq.append(cq)
             ws.append(cs)
 
+        stream = [(x_sb[0], IN // 2, 0), (x_sb[1], IN // 2, 0),
+                  (h_sb[0], H // 2, 0), (h_sb[0], H // 2, 256),
+                  (h_sb[1], H // 2, 0), (h_sb[1], H // 2, 256)]
+        pairs = [(xq[:], xs[:]), (hq[:, 0:512], hs[:, 0:512]), (hq[:, 512:1024], hs[:, 512:1024])]
+        gwords = (IN + H) // 2
+        for j in range(NBLK):
+            stream.extend([(gw_sb[j], gwords, 0), (gw_sb[j], gwords, 256), (gw_sb[j], gwords, 512),
+                           (wi_sb[j], IN // 2, 0), (wr_sb[j], H // 2, 0), (wr_sb[j], H // 2, 256)])
+            for m in range(3):
+                pairs.append((wq[j][:, m * 512:(m + 1) * 512], ws[j][:, m * 512:(m + 1) * 512]))
+
+        st = {"ti": 0, "ci": 0, "qi": 0, "fi": 0}
+        banks = {}
+        groups = {}
+
+        def tp():
+            n = st["ti"]
+            if n >= len(stream):
+                return
+            st["ti"] = n + 1
+            src, row_words, first = stream[n]
+            s32 = src[:].bitcast(F32)
+            bank = ps_t.tile([P, 2, 2 * P], F32, name="bank")
+            for t in range(2):
+                for u in range(2):
+                    c0 = t * row_words + first + u * P
+                    nc.tensor.transpose(bank[:, u, t * P:(t + 1) * P], s32[:, c0:c0 + P], ident[:])
+            banks[n] = bank
+
+        def cp(eng):
+            n = st["ci"]
+            if n >= len(stream):
+                return
+            st["ci"] = n + 1
+            if n % 2 == 0:
+                grouped = stage.tile([P, 2048], BF16, name="grouped", align_bytes=64)
+                groups[n // 2] = grouped
+            g32 = groups[n // 2][:].bitcast(F32)
+            half = n % 2
+            dst = g32[:, half * 512:(half + 1) * 512].rearrange("p (r u) -> p r u", u=2)
+            if eng == "v":
+                nc.vector.tensor_copy(out=dst, in_=banks[n][:].rearrange("p u r -> p r u"))
+            else:
+                nc.scalar.copy(out=dst, in_=banks[n][:].rearrange("p u r -> p r u"))
+
+        def q():
+            while 2 * st["qi"] + 2 <= st["ci"]:
+                k = st["qi"]
+                st["qi"] = k + 1
+                nc.vector.quantize_mx(out=pairs[k][0].bitcast(FP8X4), scales=pairs[k][1], in_=groups[k][:])
+
+        rc_bc = keep.tile([P, H], F32, name="rc_bc")
+        gb_bc = keep.tile([P, H], F32, name="gb_bc")
+        small = {}
+
+        def chain1():
+            ab = keep.tile([P, P], F32, name="ab")
+            nc.scalar.activation(out=ab[:], in_=tg[:, 0:P], func=ACT.Abs)
+            ex = keep.tile([P, P], F32, name="ex")
+            nc.scalar.activation(out=ex[:], in_=ab[:], func=ACT.Exp, scale=-1.0)
+            e1 = keep.tile([P, P], F32, name="e1")
+            nc.vector.tensor_scalar_add(out=e1[:], in0=ex[:], scalar1=1.0)
+            rl = keep.tile([P, P], F32, name="rl")
+            nc.vector.tensor_scalar_max(out=rl[:], in0=tg[:, 0:P], scalar1=0.0)
+            ln = keep.tile([P, P], F32, name="ln")
+            nc.scalar.activation(out=ln[:], in_=e1[:], func=ACT.Ln)
+            small["rl"] = rl
+            small["ln"] = ln
+
+        def chain2():
+            tp_ = keep.tile([P, P], F32, name="tp_")
+            nc.vector.scalar_tensor_tensor(out=tp_[:], in0=small["ln"][:], scalar=1.0, in1=small["rl"][:],
+                                           op0=ALU.add, op1=ALU.add)
+            rc = keep.tile([P, P], F32, name="rc")
+            nc.vector.reciprocal(out=rc[:], in_=tp_[:])
+            hi = keep.tile([P, P], BF16, name="hi")
+            nc.vector.tensor_copy(out=hi[:], in_=rc[:])
+            lo = keep.tile([P, P], BF16, name="lo")
+            nc.vector.tensor_tensor(out=lo[:], in0=rc[:], in1=hi[:], op=ALU.subtract)
+            small["hi"] = hi
+            small["lo"] = lo
+
+        def tanh_table():
+            dm = keep.tile([P, 1], F32, name="dm")
+            nc.scalar.activation(out=dm[:], in_=small["ln"][:, 0:1], func=ACT.Tanh)
+
+        spread = {}
+
+        def bcm(what, half):
+            if what == "gb":
+                ps = ps_r.tile([P, 512], F32, name="rec")
+            else:
+                ps = ps_p.tile([P, 512], F32, name="pre")
+            for k in range(4):
+                r = half * 4 + k
+                sel = identb[:, r:r + 1].to_broadcast([P, P])
+                o = ps[:, k * P:(k + 1) * P]
+                if what == "gb":
+                    nc.tensor.matmul(out=o, lhsT=sel, rhs=tg[:, P:2 * P], start=True, stop=True)
+                else:
+                    nc.tensor.matmul(out=o, lhsT=sel, rhs=small["hi"][:], start=True, stop=False)
+                    nc.tensor.matmul(out=o, lhsT=sel, rhs=small["lo"][:], start=False, stop=True)
+            spread[(what, half)] = ps
+
+        def bce(what, half):
+            dst = gb_bc if what == "gb" else rc_bc
+            nc.scalar.copy(out=dst[:, half * 512:(half + 1) * 512], in_=spread[(what, half)][:])
+
+        leak = {}
+
+        def f():
+            n = st["fi"]
+            if n >= NROUND:
+                return
+            st["fi"] = n + 1
+            j, bp = n // 2, n % 2
+            cols = slice(j * OB, (j + 1) * OB)
+            lk = keep.tile([P, 512], F32, name="leak%d" % n)
+            eng = nc.gpsimd if LEAK_ENG == "g" else nc.vector
+            eng.tensor_tensor(out=lk[:].rearrange("p (s n) -> p s n", s=2),
+                              in0=h_sb[bp][:].rearrange("p (s o) -> p s o", s=2)[:, :, cols],
+                              in1=rc_bc[:, cols].unsqueeze(1).to_broadcast([P, 2, OB]), op=ALU.mult)
+            leak[n] = lk
+
         o0_v = out_0.rearrange("(i p) o -> p i o", p=P)
         o1_v = out_1.rearrange("(i p) o -> p i o", p=P)
+        R = {}
 
-        def mx(out, a_codes, a_scales, a0, j, q, start, stop):
+        def mx(out, a_codes, a_scales, a0, j, qq, start, stop):
             nc.tensor.matmul_mx(out=out,
                                 lhsT=a_codes[:, a0:a0 + P].bitcast(FP8X4), lhsT_scale=a_scales[:, a0:a0 + P],
-                                rhs=wq[j][:, q * OB:(q + 1) * OB].bitcast(FP8X4),
-                                rhs_scale=ws[j][:, q * OB:(q + 1) * OB],
+                                rhs=wq[j][:, qq * OB:(qq + 1) * OB].bitcast(FP8X4),
+                                rhs_scale=ws[j][:, qq * OB:(qq + 1) * OB],
                                 start=start, stop=stop)
 
-        def round_(j, bp):
-            pre = ps_a.tile([P, 512], F32, name="pre")
-            rec = ps_a.tile([P, 512], F32, name="rec")
-            xin = ps_x.tile([P, 512], F32, name="xin")
+        def mx_round(r):
+            j, bp = r // 2, r % 2
+            pre = ps_p.tile([P, 512], F32, name="pre")
             for s in range(2):
                 o = pre[:, s * OB:(s + 1) * OB]
                 mx(o, xq, xs, bp * 256 + s * P, j, 0, True, False)
                 mx(o, hq, hs, bp * 512 + s * P, j, 1, False, False)
                 mx(o, hq, hs, bp * 512 + 256 + s * P, j, 2, False, True)
+            xin = ps_x.tile([P, 512], F32, name="xin")
+            for s in range(2):
+                mx(xin[:, s * OB:(s + 1) * OB], xq, xs, bp * 256 + s * P, j, 3, True, True)
+            rec = ps_r.tile([P, 512], F32, name="rec")
             for s in range(2):
                 o = rec[:, s * OB:(s + 1) * OB]
-                mx(o, hq, hs, bp * 512 + s * P, j, 3, True, False)
-                mx(o, hq, hs, bp * 512 + 256 + s * P, j, 4, False, True)
-            for s in range(2):
-                mx(xin[:, s * OB:(s + 1) * OB], xq, xs, bp * 256 + s * P, j, 5, True, True)
+                mx(o, hq, hs, bp * 512 + s * P, j, 4, True, False)
+                mx(o, hq, hs, bp * 512 + 256 + s * P, j, 5, False, True)
+            R[r] = {"pre": pre, "xin": xin, "rec": rec}
 
-            cols = slice(j * OB, (j + 1) * OB)
-            xin_sb = work.tile([P, 512], F32, name="xin_sb")
-            nc.scalar.copy(out=xin_sb[:], in_=xin[:])
-            nc.sync.dma_start(out=o0_v[:, 2 * bp:2 * bp + 2, cols], in_=xin_sb[:].rearrange("p (s n) -> p s n", s=2))
+        def split(ap):
+            return ap.rearrange("p (s n) -> p s n", s=2)
 
+        def op_b(r):
+            cols = slice((r // 2) * OB, (r // 2 + 1) * OB)
             u = work.tile([P, 512], F32, name="u")
-            nc.vector.tensor_tensor(out=u[:].rearrange("p (s n) -> p s n", s=2),
-                                    in0=pre[:].rearrange("p (s n) -> p s n", s=2),
+            nc.vector.tensor_tensor(out=split(u[:]), in0=split(R[r]["pre"][:]),
                                     in1=gb_bc[:, cols].unsqueeze(1).to_broadcast([P, 2, OB]), op=ALU.add)
-            t1 = work.tile([P, 512], F32, name="t1")
-            nc.scalar.activation(out=t1[:], in_=u[:], func=ACT.Tanh)
-            t2 = work.tile([P, 512], F32, name="t2")
-            nc.scalar.activation(out=t2[:], in_=t1[:], func=ACT.Tanh, scale=0.5)
-            m2 = work.tile([P, 512], F32, name="m2")
-            nc.vector.tensor_tensor(out=m2[:].rearrange("p (s n) -> p s n", s=2),
-                                    in0=xin_sb[:].rearrange("p (s n) -> p s n", s=2),
-                                    in1=leak[bp][:].rearrange("p (s o) -> p s o", s=2)[:, :, cols], op=ALU.subtract)
-            w = work.tile([P, 512], F32, name="w")
-            nc.vector.scalar_tensor_tensor(out=w[:], in0=t2[:], scalar=1.0, in1=rec[:], op0=ALU.add, op1=ALU.mult)
-            k1 = work.tile([P, 512], F32, name="k1")
-            nc.vector.scalar_tensor_tensor(out=k1[:], in0=w[:], scalar=0.5, in1=m2[:], op0=ALU.mult, op1=ALU.add)
-            nc.sync.dma_start(out=o1_v[:, 2 * bp:2 * bp + 2, cols], in_=k1[:].rearrange("p (s n) -> p s n", s=2))
+            R[r]["u"] = u
 
-        flip_block(0)
-        for j in range(NBLK):
-            if j + 1 < NBLK:
-                flip_block(j + 1)
-            round_(j, 0)
-            round_(j, 1)
+        def op_a(r):
+            j, bp = r // 2, r % 2
+            xin_sb = work.tile([P, 512], F32, name="xin_sb")
+            nc.scalar.copy(out=xin_sb[:], in_=R[r]["xin"][:])
+            nc.sync.dma_start(out=o0_v[:, 2 * bp:2 * bp + 2, j * OB:(j + 1) * OB], in_=split(xin_sb[:]))
+            R[r]["xin_sb"] = xin_sb
+
+        def op_g(r):
+            m2 = work.tile([P, 512], F32, name="m2")
+            eng = nc.gpsimd if G_ENG == "g" else nc.vector
+            eng.tensor_tensor(out=m2[:], in0=R[r]["xin_sb"][:], in1=leak[r][:], op=ALU.subtract)
+            R[r]["m2"] = m2
+
+        def op_c(r):
+            t1 = work.tile([P, 512], F32, name="t1")
+            nc.scalar.activation(out=t1[:], in_=R[r]["u"][:], func=ACT.Tanh)
+            R[r]["t1"] = t1
+
+        def op_d(r):
+            t2 = work.tile([P, 512], F32, name="t2")
+            nc.scalar.activation(out=t2[:], in_=R[r]["t1"][:], func=ACT.Tanh, scale=0.5)
+            R[r]["t2"] = t2
+
+        def op_e(r):
+            w = work.tile([P, 512], F32, name="w")
+            nc.vector.scalar_tensor_tensor(out=w[:], in0=R[r]["t2"][:], scalar=1.0, in1=R[r]["rec"][:],
+                                           op0=ALU.add, op1=ALU.mult)
+            R[r]["w"] = w
+
+        def op_h(r):
+            j, bp = r // 2, r % 2
+            k1 = work.tile([P, 512], F32, name="k1")
+            nc.vector.scalar_tensor_tensor(out=k1[:], in0=R[r]["w"][:], scalar=0.5, in1=R[r]["m2"][:],
+                                           op0=ALU.mult, op1=ALU.add)
+            nc.sync.dma_start(out=o1_v[:, 2 * bp:2 * bp + 2, j * OB:(j + 1) * OB], in_=split(k1[:]))
+
+        chain1()
+        bcm("gb", 0)
+        bcm("gb", 1)
+        tp()
+        tp()
+        tp()
+        cp("v")
+        tp()
+        cp("v")
+        tp()
+        q()
+        bce("gb", 0)
+        cp("s")
+        tp()
+        chain2()
+        cp("v")
+        q()
+        bcm("rc", 0)
+        bcm("rc", 1)
+        tp()
+        cp("s")
+        tp()
+        cp("v")
+        tp()
+        q()
+        tanh_table()
+        bce("rc", 0)
+        f()
+        f()
+        for k in range(6):
+            cp(W0[k])
+            tp()
+            if k % 2 == 1:
+                q()
+        mx_round(0)
+        for k in range(LEAD):
+            cp(LEAD_ENG[k])
+            tp()
+        for p in range(NROUND + 1):
+            if p < NROUND:
+                op_b(p)
+            cp("s")
+            cp("s")
+            if p == 1:
+                bce("gb", 1)
+            if p == 2:
+                bce("rc", 1)
+            if p > 0:
+                op_e(p - 1)
+                op_h(p - 1)
+            if p < NROUND:
+                op_a(p)
+                op_g(p)
+                f()
+                op_c(p)
+                op_d(p)
+            tp()
+            tp()
+            q()
+            cp(VCP[p] if p < NROUND else "v")
+            q()
+            if p + 1 < NROUND:
+                mx_round(p + 1)
+            tp()

@@ -19,12 +19,12 @@ NROUND = 2 * NBLK
 FLOPS = 2 * B * H * (IN + IN + H + H)
 
 PIN = True
-LEAK_ENG = "g"
-G_ENG = "g"
-LEAD = 2
-LEAD_ENG = "ss"
-VCP = "vvvvvvvv"
-W0 = "vsvsvs"
+HEAD = ["kT", "k1a", "cV", "cV", "k1b", "q", "cS", "cV", "k2", "cS", "cV", "q", "cS", "cV", "cS", "q", "cV", "cS", "q", "cV", "q", "sig", "M0", "cS", "cS", "cS"]
+CAP = 15
+AHEAD = 5
+AHEAD2 = 3
+VCP = "vsvsvsvs"
+LOOP = "A"
 
 
 def tile_ltccell_pa_kernel(tc, x, h, tau, W_in, W_rec, gate_w, gate_b, out_0, out_1):
@@ -32,23 +32,19 @@ def tile_ltccell_pa_kernel(tc, x, h, tau, W_in, W_rec, gate_w, gate_b, out_0, ou
     with ExitStack() as ctx:
         keep = ctx.enter_context(tc.tile_pool(name="keep", bufs=1))
         stage = ctx.enter_context(tc.tile_pool(name="stage", bufs=4))
-        work = ctx.enter_context(tc.tile_pool(name="work", bufs=4))
-        ps_t = ctx.enter_context(tc.psum_pool(name="ps_t", bufs=3))
-        ps_p = ctx.enter_context(tc.psum_pool(name="ps_p", bufs=2))
-        ps_r = ctx.enter_context(tc.psum_pool(name="ps_r", bufs=2))
-        ps_x = ctx.enter_context(tc.psum_pool(name="ps_x", bufs=1))
+        work = ctx.enter_context(tc.tile_pool(name="work", bufs=3))
+        outp = ctx.enter_context(tc.tile_pool(name="outp", bufs=4))
+        ps = ctx.enter_context(tc.psum_pool(name="ps", bufs=8))
         if PIN:
             ctx.enter_context(tc.manual_schedule())
 
         ident = keep.tile([P, P], F32, name="ident")
         make_identity(nc, ident[:])
-        identb = keep.tile([P, P], BF16, name="identb")
-        make_identity(nc, identb[:])
 
         tg = keep.tile([P, 2 * P], BF16, name="tg")
         nc.vector.memset(tg[:], 0.0)
-        nc.sync.dma_start(out=tg[0:8, 0:P], in_=tau.rearrange("(r c) -> r c", c=P))
-        nc.sync.dma_start(out=tg[0:8, P:2 * P], in_=gate_b.rearrange("(r c) -> r c", c=P))
+        nc.sync.dma_start(out=tg[0:4, :], in_=tau.rearrange("(a c) -> a c", c=OB))
+        nc.sync.dma_start(out=tg[4:8, :], in_=gate_b.rearrange("(a c) -> a c", c=OB))
 
         x_v = x.rearrange("(i p) k -> p i k", p=P)
         h_v = h.rearrange("(i p) k -> p i k", p=P)
@@ -62,17 +58,15 @@ def tile_ltccell_pa_kernel(tc, x, h, tau, W_in, W_rec, gate_w, gate_b, out_0, ou
             nc.sync.dma_start(out=ht[:].rearrange("p (i k) -> p i k", i=2), in_=h_v[:, 2 * bp:2 * bp + 2, :])
             h_sb.append(ht)
 
-        g_v = gate_w.rearrange("(t p) k -> p t k", p=P)
-        r_v = W_rec.rearrange("(t p) k -> p t k", p=P)
-        i_v = W_in.rearrange("(t p) k -> p t k", p=P)
         gw_sb, wr_sb, wi_sb = [], [], []
-        for j in range(NBLK):
-            gt = keep.tile([P, 2 * (IN + H)], BF16, name="gw_sb%d" % j)
-            nc.sync.dma_start(out=gt[:].rearrange("p (t k) -> p t k", t=2), in_=g_v[:, 2 * j:2 * j + 2, :])
-            it = keep.tile([P, 2 * IN], BF16, name="wi_sb%d" % j)
-            nc.sync.dma_start(out=it[:].rearrange("p (t k) -> p t k", t=2), in_=i_v[:, 2 * j:2 * j + 2, :])
-            rt = keep.tile([P, 2 * H], BF16, name="wr_sb%d" % j)
-            nc.sync.dma_start(out=rt[:].rearrange("p (t k) -> p t k", t=2), in_=r_v[:, 2 * j:2 * j + 2, :])
+        for a in range(NBLK):
+            rows = slice(a * OB, (a + 1) * OB)
+            gt = keep.tile([P, 2 * (IN + H)], BF16, name="gw_sb%d" % a)
+            nc.sync.dma_start(out=gt[:], in_=gate_w[rows, :].rearrange("(p e) k -> p (e k)", e=2))
+            it = keep.tile([P, 2 * IN], BF16, name="wi_sb%d" % a)
+            nc.sync.dma_start(out=it[:], in_=W_in[rows, :].rearrange("(p e) k -> p (e k)", e=2))
+            rt = keep.tile([P, 2 * H], BF16, name="wr_sb%d" % a)
+            nc.sync.dma_start(out=rt[:], in_=W_rec[rows, :].rearrange("(p e) k -> p (e k)", e=2))
             gw_sb.append(gt)
             wr_sb.append(rt)
             wi_sb.append(it)
@@ -81,273 +75,259 @@ def tile_ltccell_pa_kernel(tc, x, h, tau, W_in, W_rec, gate_w, gate_b, out_0, ou
         xs = keep.tile([P, 512], U8, name="xs", align_bytes=64)
         hq = keep.tile([P, 1024], U32, name="hq", align_bytes=64)
         hs = keep.tile([P, 1024], U8, name="hs", align_bytes=64)
+        hg = []
+        for g in range(2):
+            hgt = keep.tile([P, 2048], BF16, name="hg%d" % g, align_bytes=64)
+            hg.append(hgt)
         wq, ws = [], []
-        for j in range(NBLK):
-            cq = keep.tile([P, 6 * OB], U32, name="wq%d" % j, align_bytes=64)
-            cs = keep.tile([P, 6 * OB], U8, name="ws%d" % j, align_bytes=64)
+        for a in range(NBLK):
+            cq = keep.tile([P, 6 * OB], U32, name="wq%d" % a, align_bytes=64)
+            cs = keep.tile([P, 6 * OB], U8, name="ws%d" % a, align_bytes=64)
             wq.append(cq)
             ws.append(cs)
 
-        stream = [(x_sb[0], IN // 2, 0), (x_sb[1], IN // 2, 0),
-                  (h_sb[0], H // 2, 0), (h_sb[0], H // 2, 256),
-                  (h_sb[1], H // 2, 0), (h_sb[1], H // 2, 256)]
-        pairs = [(xq[:], xs[:]), (hq[:, 0:512], hs[:, 0:512]), (hq[:, 512:1024], hs[:, 512:1024])]
+        stream = [(x_sb[0], IN // 2, 0, "x", 0, []), (x_sb[1], IN // 2, 0, "x", 1, ["x"]),
+                  (h_sb[0], H // 2, 0, "h0", 0, []), (h_sb[0], H // 2, 256, "h1", 0, []),
+                  (h_sb[1], H // 2, 0, "h0", 1, ["h0"]), (h_sb[1], H // 2, 256, "h1", 1, ["h1"])]
+        dest = {"x": (xq[:], xs[:]), "h0": (hq[:, 0:512], hs[:, 0:512]), "h1": (hq[:, 512:1024], hs[:, 512:1024])}
         gwords = (IN + H) // 2
-        for j in range(NBLK):
-            stream.extend([(gw_sb[j], gwords, 0), (gw_sb[j], gwords, 256), (gw_sb[j], gwords, 512),
-                           (wi_sb[j], IN // 2, 0), (wr_sb[j], H // 2, 0), (wr_sb[j], H // 2, 256)])
-            for m in range(3):
-                pairs.append((wq[j][:, m * 512:(m + 1) * 512], ws[j][:, m * 512:(m + 1) * 512]))
+        for a in range(NBLK):
+            srcs = [(gw_sb[a], gwords, 0), (gw_sb[a], gwords, 256), (gw_sb[a], gwords, 512),
+                    (wi_sb[a], IN // 2, 0), (wr_sb[a], H // 2, 0), (wr_sb[a], H // 2, 256)]
+            for m in range(6):
+                key = "w%d_%d" % (a, m // 2)
+                stream.append((srcs[m][0], srcs[m][1], srcs[m][2], key, m % 2, [key] if m % 2 == 1 else []))
+                dest[key] = (wq[a][:, (m // 2) * 512:(m // 2 + 1) * 512], ws[a][:, (m // 2) * 512:(m // 2 + 1) * 512])
 
-        st = {"ti": 0, "ci": 0, "qi": 0, "fi": 0}
+        st = {"ti": 0, "ci": 0, "qi": 0, "cap": CAP, "ahead": AHEAD}
         banks = {}
-        groups = {}
+        groups = {"h0": hg[0], "h1": hg[1]}
+        ready = []
 
         def tp():
             n = st["ti"]
-            if n >= len(stream):
-                return
             st["ti"] = n + 1
-            src, row_words, first = stream[n]
+            src, row_words, first = stream[n][0:3]
             s32 = src[:].bitcast(F32)
-            bank = ps_t.tile([P, 2, 2 * P], F32, name="bank")
-            for t in range(2):
+            bank = ps.tile([P, 512], F32, name="bank")
+            for e in range(2):
                 for u in range(2):
-                    c0 = t * row_words + first + u * P
-                    nc.tensor.transpose(bank[:, u, t * P:(t + 1) * P], s32[:, c0:c0 + P], ident[:])
+                    c0 = e * row_words + first + u * P
+                    nc.tensor.transpose(bank[:, u * OB + e * P:u * OB + (e + 1) * P], s32[:, c0:c0 + P], ident[:])
             banks[n] = bank
+
+        def fill():
+            while st["ti"] - st["ci"] < st["ahead"] and st["ti"] < min(len(stream), st["cap"]):
+                tp()
 
         def cp(eng):
             n = st["ci"]
             if n >= len(stream):
                 return
+            if st["ti"] <= n:
+                tp()
             st["ci"] = n + 1
-            if n % 2 == 0:
+            key, half, done = stream[n][3:6]
+            if key not in groups:
                 grouped = stage.tile([P, 2048], BF16, name="grouped", align_bytes=64)
-                groups[n // 2] = grouped
-            g32 = groups[n // 2][:].bitcast(F32)
-            half = n % 2
+                groups[key] = grouped
+            g32 = groups[key][:].bitcast(F32)
             dst = g32[:, half * 512:(half + 1) * 512].rearrange("p (r u) -> p r u", u=2)
+            src = banks[n][:].rearrange("p (u r) -> p r u", u=2)
             if eng == "v":
-                nc.vector.tensor_copy(out=dst, in_=banks[n][:].rearrange("p u r -> p r u"))
+                nc.vector.tensor_copy(out=dst, in_=src)
             else:
-                nc.scalar.copy(out=dst, in_=banks[n][:].rearrange("p u r -> p r u"))
+                nc.scalar.copy(out=dst, in_=src)
+            ready.extend(done)
 
         def q():
-            while 2 * st["qi"] + 2 <= st["ci"]:
-                k = st["qi"]
-                st["qi"] = k + 1
-                nc.vector.quantize_mx(out=pairs[k][0].bitcast(FP8X4), scales=pairs[k][1], in_=groups[k][:])
+            while st["qi"] < len(ready):
+                key = ready[st["qi"]]
+                st["qi"] = st["qi"] + 1
+                nc.vector.quantize_mx(out=dest[key][0].bitcast(FP8X4), scales=dest[key][1], in_=groups[key][:])
 
-        rc_bc = keep.tile([P, H], F32, name="rc_bc")
-        gb_bc = keep.tile([P, H], F32, name="gb_bc")
         small = {}
 
-        def chain1():
-            ab = keep.tile([P, P], F32, name="ab")
-            nc.scalar.activation(out=ab[:], in_=tg[:, 0:P], func=ACT.Abs)
-            ex = keep.tile([P, P], F32, name="ex")
+        def chain_t():
+            bank = ps.tile([P, 512], F32, name="bank")
+            nc.tensor.transpose(bank[:, 0:P], tg[:].bitcast(F32), ident[:])
+            small["bank"] = bank
+
+        def chain_1a():
+            tb = keep.tile([P, 8], F32, name="tb")
+            nc.vector.tensor_copy(out=tb[:], in_=small["bank"][:, 0:8])
+            tbv = tb[:].bitcast(BF16)
+            ab = keep.tile([P, 8], F32, name="ab")
+            nc.scalar.activation(out=ab[:], in_=tbv[:, 0:8], func=ACT.Abs)
+            ex = keep.tile([P, 8], F32, name="ex")
             nc.scalar.activation(out=ex[:], in_=ab[:], func=ACT.Exp, scale=-1.0)
-            e1 = keep.tile([P, P], F32, name="e1")
-            nc.vector.tensor_scalar_add(out=e1[:], in0=ex[:], scalar1=1.0)
-            rl = keep.tile([P, P], F32, name="rl")
-            nc.vector.tensor_scalar_max(out=rl[:], in0=tg[:, 0:P], scalar1=0.0)
-            ln = keep.tile([P, P], F32, name="ln")
+            small["tbv"] = tbv
+            small["ex"] = ex
+
+        def chain_1b():
+            e1 = keep.tile([P, 8], F32, name="e1")
+            nc.vector.tensor_scalar_add(out=e1[:], in0=small["ex"][:], scalar1=1.0)
+            rl = keep.tile([P, 8], F32, name="rl")
+            nc.vector.tensor_scalar_max(out=rl[:], in0=small["tbv"][:, 0:8], scalar1=0.0)
+            gbf = keep.tile([P, 8], F32, name="gbf")
+            nc.vector.tensor_copy(out=gbf[:], in_=small["tbv"][:, 8:16])
+            ln = keep.tile([P, 8], F32, name="ln")
             nc.scalar.activation(out=ln[:], in_=e1[:], func=ACT.Ln)
             small["rl"] = rl
+            small["gbf"] = gbf
             small["ln"] = ln
 
-        def chain2():
-            tp_ = keep.tile([P, P], F32, name="tp_")
+        def chain_2():
+            tp_ = keep.tile([P, 8], F32, name="tp_")
             nc.vector.scalar_tensor_tensor(out=tp_[:], in0=small["ln"][:], scalar=1.0, in1=small["rl"][:],
                                            op0=ALU.add, op1=ALU.add)
-            rc = keep.tile([P, P], F32, name="rc")
+            rc = keep.tile([P, 8], F32, name="rc")
             nc.vector.reciprocal(out=rc[:], in_=tp_[:])
-            hi = keep.tile([P, P], BF16, name="hi")
-            nc.vector.tensor_copy(out=hi[:], in_=rc[:])
-            lo = keep.tile([P, P], BF16, name="lo")
-            nc.vector.tensor_tensor(out=lo[:], in0=rc[:], in1=hi[:], op=ALU.subtract)
-            small["hi"] = hi
-            small["lo"] = lo
+            nrc = keep.tile([P, 8], F32, name="nrc")
+            nc.vector.tensor_scalar_mul(out=nrc[:], in0=rc[:], scalar1=-1.0)
+            small["nrc"] = nrc
 
-        def tanh_table():
+        def sig_table():
             dm = keep.tile([P, 1], F32, name="dm")
-            nc.scalar.activation(out=dm[:], in_=small["ln"][:, 0:1], func=ACT.Tanh)
-
-        spread = {}
-
-        def bcm(what, half):
-            if what == "gb":
-                ps = ps_r.tile([P, 512], F32, name="rec")
-            else:
-                ps = ps_p.tile([P, 512], F32, name="pre")
-            for k in range(4):
-                r = half * 4 + k
-                sel = identb[:, r:r + 1].to_broadcast([P, P])
-                o = ps[:, k * P:(k + 1) * P]
-                if what == "gb":
-                    nc.tensor.matmul(out=o, lhsT=sel, rhs=tg[:, P:2 * P], start=True, stop=True)
-                else:
-                    nc.tensor.matmul(out=o, lhsT=sel, rhs=small["hi"][:], start=True, stop=False)
-                    nc.tensor.matmul(out=o, lhsT=sel, rhs=small["lo"][:], start=False, stop=True)
-            spread[(what, half)] = ps
-
-        def bce(what, half):
-            dst = gb_bc if what == "gb" else rc_bc
-            nc.scalar.copy(out=dst[:, half * 512:(half + 1) * 512], in_=spread[(what, half)][:])
-
-        leak = {}
-
-        def f():
-            n = st["fi"]
-            if n >= NROUND:
-                return
-            st["fi"] = n + 1
-            j, bp = n // 2, n % 2
-            cols = slice(j * OB, (j + 1) * OB)
-            lk = keep.tile([P, 512], F32, name="leak%d" % n)
-            eng = nc.gpsimd if LEAK_ENG == "g" else nc.vector
-            eng.tensor_tensor(out=lk[:].rearrange("p (s n) -> p s n", s=2),
-                              in0=h_sb[bp][:].rearrange("p (s o) -> p s o", s=2)[:, :, cols],
-                              in1=rc_bc[:, cols].unsqueeze(1).to_broadcast([P, 2, OB]), op=ALU.mult)
-            leak[n] = lk
+            nc.scalar.activation(out=dm[:], in_=small["ln"][:, 0:1], func=ACT.Sigmoid)
 
         o0_v = out_0.rearrange("(i p) o -> p i o", p=P)
         o1_v = out_1.rearrange("(i p) o -> p i o", p=P)
         R = {}
-
-        def mx(out, a_codes, a_scales, a0, j, qq, start, stop):
-            nc.tensor.matmul_mx(out=out,
-                                lhsT=a_codes[:, a0:a0 + P].bitcast(FP8X4), lhsT_scale=a_scales[:, a0:a0 + P],
-                                rhs=wq[j][:, qq * OB:(qq + 1) * OB].bitcast(FP8X4),
-                                rhs_scale=ws[j][:, qq * OB:(qq + 1) * OB],
-                                start=start, stop=stop)
+        K = {}
 
         def mx_round(r):
-            j, bp = r // 2, r % 2
-            pre = ps_p.tile([P, 512], F32, name="pre")
+            a, e = r // 2, r % 2
+            pre = ps.tile([P, 512], F32, name="bank")
+            rec = None
+            plan = [(pre, 0, xq[:], xs[:], True, False), (pre, 1, hq[:, 0:512], hs[:, 0:512], False, False),
+                    (pre, 2, hq[:, 512:1024], hs[:, 512:1024], False, True)]
+            for o, qq, rc_, rs_, start, stop in plan:
+                w0 = qq * OB + e * P
+                nc.tensor.matmul_mx(out=o[:], lhsT=wq[a][:, w0:w0 + P].bitcast(FP8X4), lhsT_scale=ws[a][:, w0:w0 + P],
+                                    rhs=rc_.bitcast(FP8X4), rhs_scale=rs_, start=start, stop=stop)
+            rec = ps.tile([P, 512], F32, name="bank")
+            plan = [(rec, 4, hq[:, 0:512], hs[:, 0:512], True, False), (rec, 5, hq[:, 512:1024], hs[:, 512:1024], False, True)]
+            for o, qq, rc_, rs_, start, stop in plan:
+                w0 = qq * OB + e * P
+                nc.tensor.matmul_mx(out=o[:], lhsT=wq[a][:, w0:w0 + P].bitcast(FP8X4), lhsT_scale=ws[a][:, w0:w0 + P],
+                                    rhs=rc_.bitcast(FP8X4), rhs_scale=rs_, start=start, stop=stop)
+            R[r] = {"pre": pre, "rec": rec}
+
+        def mx_xin(k):
+            a, bp = k // 2, k % 2
+            xin = ps.tile([P, 512], F32, name="bank")
             for s in range(2):
-                o = pre[:, s * OB:(s + 1) * OB]
-                mx(o, xq, xs, bp * 256 + s * P, j, 0, True, False)
-                mx(o, hq, hs, bp * 512 + s * P, j, 1, False, False)
-                mx(o, hq, hs, bp * 512 + 256 + s * P, j, 2, False, True)
-            xin = ps_x.tile([P, 512], F32, name="xin")
-            for s in range(2):
-                mx(xin[:, s * OB:(s + 1) * OB], xq, xs, bp * 256 + s * P, j, 3, True, True)
-            rec = ps_r.tile([P, 512], F32, name="rec")
-            for s in range(2):
-                o = rec[:, s * OB:(s + 1) * OB]
-                mx(o, hq, hs, bp * 512 + s * P, j, 4, True, False)
-                mx(o, hq, hs, bp * 512 + 256 + s * P, j, 5, False, True)
-            R[r] = {"pre": pre, "xin": xin, "rec": rec}
+                b0 = (2 * bp + s) * P
+                nc.tensor.matmul_mx(out=xin[:, s * OB:(s + 1) * OB],
+                                    lhsT=xq[:, b0:b0 + P].bitcast(FP8X4), lhsT_scale=xs[:, b0:b0 + P],
+                                    rhs=wq[a][:, 3 * OB:4 * OB].bitcast(FP8X4), rhs_scale=ws[a][:, 3 * OB:4 * OB],
+                                    start=True, stop=True)
+            K[k] = {"xin": xin}
 
-        def split(ap):
-            return ap.rearrange("p (s n) -> p s n", s=2)
+        def natural(ap):
+            return ap.rearrange("q (s p e) -> q s p e", s=2, e=2)
 
-        def op_b(r):
-            cols = slice((r // 2) * OB, (r // 2 + 1) * OB)
-            u = work.tile([P, 512], F32, name="u")
-            nc.vector.tensor_tensor(out=split(u[:]), in0=split(R[r]["pre"][:]),
-                                    in1=gb_bc[:, cols].unsqueeze(1).to_broadcast([P, 2, OB]), op=ALU.add)
-            R[r]["u"] = u
-
-        def op_a(r):
-            j, bp = r // 2, r % 2
-            xin_sb = work.tile([P, 512], F32, name="xin_sb")
-            nc.scalar.copy(out=xin_sb[:], in_=R[r]["xin"][:])
-            nc.sync.dma_start(out=o0_v[:, 2 * bp:2 * bp + 2, j * OB:(j + 1) * OB], in_=split(xin_sb[:]))
-            R[r]["xin_sb"] = xin_sb
-
-        def op_g(r):
-            m2 = work.tile([P, 512], F32, name="m2")
-            eng = nc.gpsimd if G_ENG == "g" else nc.vector
-            eng.tensor_tensor(out=m2[:], in0=R[r]["xin_sb"][:], in1=leak[r][:], op=ALU.subtract)
-            R[r]["m2"] = m2
+        def by_parity(ap):
+            return ap.rearrange("q (s e p) -> q s p e", s=2, e=2)
 
         def op_c(r):
             t1 = work.tile([P, 512], F32, name="t1")
-            nc.scalar.activation(out=t1[:], in_=R[r]["u"][:], func=ACT.Tanh)
+            nc.scalar.activation(out=t1[:], in_=R[r]["pre"][:], func=ACT.Tanh, bias=small["gbf"][:, r:r + 1])
             R[r]["t1"] = t1
 
         def op_d(r):
-            t2 = work.tile([P, 512], F32, name="t2")
-            nc.scalar.activation(out=t2[:], in_=R[r]["t1"][:], func=ACT.Tanh, scale=0.5)
-            R[r]["t2"] = t2
+            gt_ = work.tile([P, 512], F32, name="gt_")
+            nc.scalar.activation(out=gt_[:], in_=R[r]["t1"][:], func=ACT.Sigmoid)
+            R[r]["gt"] = gt_
 
-        def op_e(r):
+        def op_v1(r):
             w = work.tile([P, 512], F32, name="w")
-            nc.vector.scalar_tensor_tensor(out=w[:], in0=R[r]["t2"][:], scalar=1.0, in1=R[r]["rec"][:],
-                                           op0=ALU.add, op1=ALU.mult)
+            nc.vector.tensor_tensor(out=w[:], in0=R[r]["gt"][:], in1=R[r]["rec"][:], op=ALU.mult)
             R[r]["w"] = w
 
-        def op_h(r):
-            j, bp = r // 2, r % 2
-            k1 = work.tile([P, 512], F32, name="k1")
-            nc.vector.scalar_tensor_tensor(out=k1[:], in0=R[r]["w"][:], scalar=0.5, in1=R[r]["m2"][:],
+        def op_v2(r):
+            a, e = r // 2, r % 2
+            hT = hg[a // 2][:].rearrange("p (b t) -> p b t", t=4)[:, :, 2 * (a % 2) + e]
+            w2 = outp.tile([P, 512], F32, name="w2")
+            nc.vector.scalar_tensor_tensor(out=w2[:], in0=hT, scalar=small["nrc"][:, r:r + 1], in1=R[r]["w"][:],
                                            op0=ALU.mult, op1=ALU.add)
-            nc.sync.dma_start(out=o1_v[:, 2 * bp:2 * bp + 2, j * OB:(j + 1) * OB], in_=split(k1[:]))
+            R[r]["w2"] = w2
 
-        chain1()
-        bcm("gb", 0)
-        bcm("gb", 1)
-        tp()
-        tp()
-        tp()
-        cp("v")
-        tp()
-        cp("v")
-        tp()
-        q()
-        bce("gb", 0)
-        cp("s")
-        tp()
-        chain2()
-        cp("v")
-        q()
-        bcm("rc", 0)
-        bcm("rc", 1)
-        tp()
-        cp("s")
-        tp()
-        cp("v")
-        tp()
-        q()
-        tanh_table()
-        bce("rc", 0)
-        f()
-        f()
-        for k in range(6):
-            cp(W0[k])
-            tp()
-            if k % 2 == 1:
+        def op_bt(k):
+            a, bp = k // 2, k % 2
+            wb = ps.tile([P, 512], F32, name="bank")
+            for s in range(2):
+                for e in range(2):
+                    b0 = (2 * bp + s) * P
+                    c0 = (2 * s + e) * P
+                    nc.tensor.transpose(wb[:, c0:c0 + P], R[2 * a + e]["w2"][:, b0:b0 + P], ident[:])
+            K[k]["wb"] = wb
+
+        def op_a(k):
+            a, bp = k // 2, k % 2
+            xin_sb = outp.tile([P, 512], F32, name="xin_sb")
+            nc.scalar.copy(out=natural(xin_sb[:]), in_=by_parity(K[k]["xin"][:]))
+            nc.sync.dma_start(out=o0_v[:, 2 * bp:2 * bp + 2, a * OB:(a + 1) * OB],
+                              in_=xin_sb[:].rearrange("q (s n) -> q s n", s=2))
+            K[k]["xin_sb"] = xin_sb
+
+        def op_h(k):
+            a, bp = k // 2, k % 2
+            k1 = outp.tile([P, 512], F32, name="k1")
+            nc.vector.tensor_tensor(out=natural(k1[:]), in0=by_parity(K[k]["wb"][:]), in1=natural(K[k]["xin_sb"][:]),
+                                    op=ALU.add)
+            nc.sync.dma_start(out=o1_v[:, 2 * bp:2 * bp + 2, a * OB:(a + 1) * OB],
+                              in_=k1[:].rearrange("q (s n) -> q s n", s=2))
+
+        for t in HEAD:
+            if t == "kT":
+                chain_t()
+            elif t == "k1a":
+                chain_1a()
+            elif t == "k1b":
+                chain_1b()
+            elif t == "k2":
+                chain_2()
+            elif t == "sig":
+                sig_table()
+            elif t == "cV":
+                fill()
+                cp("v")
+                fill()
+            elif t == "cS":
+                fill()
+                cp("s")
+                fill()
+            elif t == "q":
                 q()
-        mx_round(0)
-        for k in range(LEAD):
-            cp(LEAD_ENG[k])
-            tp()
-        for p in range(NROUND + 1):
+            elif t == "M0":
+                mx_round(0)
+                mx_xin(0)
+                st["cap"] = len(stream)
+                st["ahead"] = AHEAD2
+
+        for p in range(NROUND + 3):
+            if 1 <= p <= NROUND:
+                op_v1(p - 1)
+                op_v2(p - 1)
+            q()
+            if p >= 3:
+                op_bt(p - 3)
+            if LOOP == "A":
+                cp("s")
+                cp("s")
             if p < NROUND:
-                op_b(p)
-            cp("s")
-            cp("s")
-            if p == 1:
-                bce("gb", 1)
-            if p == 2:
-                bce("rc", 1)
-            if p > 0:
-                op_e(p - 1)
-                op_h(p - 1)
-            if p < NROUND:
-                op_a(p)
-                op_g(p)
-                f()
                 op_c(p)
                 op_d(p)
-            tp()
-            tp()
-            q()
-            cp(VCP[p] if p < NROUND else "v")
-            q()
+                op_a(p)
+            if LOOP == "B":
+                cp("s")
+                cp("s")
+            cp(VCP[p] if p < NROUND else "s")
+            if p >= 3:
+                op_h(p - 3)
+            fill()
             if p + 1 < NROUND:
                 mx_round(p + 1)
-            tp()
+                mx_xin(p + 1)

@@ -19,7 +19,7 @@ NROUND = 2 * NBLK
 FLOPS = 2 * B * H * (IN + IN + H + H)
 
 PIN = True
-HEAD = ["kT", "k1a", "cV", "cV", "k1b", "q", "cS", "cV", "k2", "cS", "cV", "q", "cS", "cV", "cS", "q", "cV", "cS", "q", "cV", "q", "sig", "M0", "cS", "cS", "cS"]
+HEAD = ["kT", "k1a", "cV", "cV", "k1b", "q", "cS", "cV", "k2", "cS", "cV", "q", "sig", "cV", "cS", "cV", "q", "cS", "q", "M0p", "cS", "cV", "q", "M0r", "M0x", "cS", "cS", "q", "cS", "C0"]
 CAP = 15
 AHEAD = 5
 AHEAD2 = 3
@@ -91,13 +91,20 @@ def tile_ltccell_pa_kernel(tc, x, h, tau, W_in, W_rec, gate_w, gate_b, out_0, ou
                   (h_sb[1], H // 2, 0, "h0", 1, ["h0"]), (h_sb[1], H // 2, 256, "h1", 1, ["h1"])]
         dest = {"x": (xq[:], xs[:]), "h0": (hq[:, 0:512], hs[:, 0:512]), "h1": (hq[:, 512:1024], hs[:, 512:1024])}
         gwords = (IN + H) // 2
+        narrow = []
         for a in range(NBLK):
             srcs = [(gw_sb[a], gwords, 0), (gw_sb[a], gwords, 256), (gw_sb[a], gwords, 512),
                     (wi_sb[a], IN // 2, 0), (wr_sb[a], H // 2, 0), (wr_sb[a], H // 2, 256)]
             for m in range(6):
-                key = "w%d_%d" % (a, m // 2)
-                stream.append((srcs[m][0], srcs[m][1], srcs[m][2], key, m % 2, [key] if m % 2 == 1 else []))
-                dest[key] = (wq[a][:, (m // 2) * 512:(m // 2 + 1) * 512], ws[a][:, (m // 2) * 512:(m // 2 + 1) * 512])
+                if a == 0 and m // 2 == 1:
+                    key = "w0_1_%d" % (m % 2)
+                    stream.append((srcs[m][0], srcs[m][1], srcs[m][2], key, 0, [key]))
+                    dest[key] = (wq[a][:, m * OB:(m + 1) * OB], ws[a][:, m * OB:(m + 1) * OB])
+                    narrow.append(key)
+                else:
+                    key = "w%d_%d" % (a, m // 2)
+                    stream.append((srcs[m][0], srcs[m][1], srcs[m][2], key, m % 2, [key] if m % 2 == 1 else []))
+                    dest[key] = (wq[a][:, (m // 2) * 512:(m // 2 + 1) * 512], ws[a][:, (m // 2) * 512:(m // 2 + 1) * 512])
 
         st = {"ti": 0, "ci": 0, "qi": 0, "cap": CAP, "ahead": AHEAD}
         banks = {}
@@ -144,7 +151,8 @@ def tile_ltccell_pa_kernel(tc, x, h, tau, W_in, W_rec, gate_w, gate_b, out_0, ou
             while st["qi"] < len(ready):
                 key = ready[st["qi"]]
                 st["qi"] = st["qi"] + 1
-                nc.vector.quantize_mx(out=dest[key][0].bitcast(FP8X4), scales=dest[key][1], in_=groups[key][:])
+                width = 1024 if key in narrow else 2048
+                nc.vector.quantize_mx(out=dest[key][0].bitcast(FP8X4), scales=dest[key][1], in_=groups[key][:, 0:width])
 
         small = {}
 
@@ -196,23 +204,26 @@ def tile_ltccell_pa_kernel(tc, x, h, tau, W_in, W_rec, gate_w, gate_b, out_0, ou
         R = {}
         K = {}
 
-        def mx_round(r):
+        def mx_pre(r):
             a, e = r // 2, r % 2
             pre = ps.tile([P, 512], F32, name="bank")
-            rec = None
             plan = [(pre, 0, xq[:], xs[:], True, False), (pre, 1, hq[:, 0:512], hs[:, 0:512], False, False),
                     (pre, 2, hq[:, 512:1024], hs[:, 512:1024], False, True)]
             for o, qq, rc_, rs_, start, stop in plan:
                 w0 = qq * OB + e * P
                 nc.tensor.matmul_mx(out=o[:], lhsT=wq[a][:, w0:w0 + P].bitcast(FP8X4), lhsT_scale=ws[a][:, w0:w0 + P],
                                     rhs=rc_.bitcast(FP8X4), rhs_scale=rs_, start=start, stop=stop)
+            R[r] = {"pre": pre}
+
+        def mx_rec(r):
+            a, e = r // 2, r % 2
             rec = ps.tile([P, 512], F32, name="bank")
             plan = [(rec, 4, hq[:, 0:512], hs[:, 0:512], True, False), (rec, 5, hq[:, 512:1024], hs[:, 512:1024], False, True)]
             for o, qq, rc_, rs_, start, stop in plan:
                 w0 = qq * OB + e * P
                 nc.tensor.matmul_mx(out=o[:], lhsT=wq[a][:, w0:w0 + P].bitcast(FP8X4), lhsT_scale=ws[a][:, w0:w0 + P],
                                     rhs=rc_.bitcast(FP8X4), rhs_scale=rs_, start=start, stop=stop)
-            R[r] = {"pre": pre, "rec": rec}
+            R[r]["rec"] = rec
 
         def mx_xin(k):
             a, bp = k // 2, k % 2
@@ -253,6 +264,19 @@ def tile_ltccell_pa_kernel(tc, x, h, tau, W_in, W_rec, gate_w, gate_b, out_0, ou
             nc.vector.scalar_tensor_tensor(out=w2[:], in0=hT, scalar=small["nrc"][:, r:r + 1], in1=R[r]["w"][:],
                                            op0=ALU.mult, op1=ALU.add)
             R[r]["w2"] = w2
+
+        def op_v12_half(r, half):
+            a, e = r // 2, r % 2
+            cols = slice(half * OB, (half + 1) * OB)
+            if half == 0:
+                w = work.tile([P, 512], F32, name="w")
+                w2 = outp.tile([P, 512], F32, name="w2")
+                R[r]["w"] = w
+                R[r]["w2"] = w2
+            hT = hg[a // 2][:].rearrange("p (b t) -> p b t", t=4)[:, cols, 2 * (a % 2) + e]
+            nc.vector.tensor_tensor(out=R[r]["w"][:, cols], in0=R[r]["gt"][:, cols], in1=R[r]["rec"][:, cols], op=ALU.mult)
+            nc.vector.scalar_tensor_tensor(out=R[r]["w2"][:, cols], in0=hT, scalar=small["nrc"][:, r:r + 1],
+                                           in1=R[r]["w"][:, cols], op0=ALU.mult, op1=ALU.add)
 
         def op_bt(k):
             a, bp = k // 2, k % 2
@@ -301,33 +325,62 @@ def tile_ltccell_pa_kernel(tc, x, h, tau, W_in, W_rec, gate_w, gate_b, out_0, ou
                 fill()
             elif t == "q":
                 q()
-            elif t == "M0":
-                mx_round(0)
+            elif t == "M0p":
+                mx_pre(0)
+            elif t == "M0r":
+                mx_rec(0)
+            elif t == "M0x":
                 mx_xin(0)
                 st["cap"] = len(stream)
                 st["ahead"] = AHEAD2
+            elif t == "C0":
+                op_c(0)
+                op_d(0)
+        op_a(0)
 
-        for p in range(NROUND + 3):
-            if 1 <= p <= NROUND:
+        for p in range(6):
+            q()
+            if p >= 1:
                 op_v1(p - 1)
                 op_v2(p - 1)
-            q()
             if p >= 3:
                 op_bt(p - 3)
-            if LOOP == "A":
-                cp("s")
-                cp("s")
-            if p < NROUND:
+            cp("s")
+            cp("s")
+            if p > 0:
                 op_c(p)
                 op_d(p)
                 op_a(p)
-            if LOOP == "B":
-                cp("s")
-                cp("s")
-            cp(VCP[p] if p < NROUND else "s")
+            cp(VCP[p])
+            q()
             if p >= 3:
                 op_h(p - 3)
             fill()
-            if p + 1 < NROUND:
-                mx_round(p + 1)
-                mx_xin(p + 1)
+            mx_pre(p + 1)
+            mx_rec(p + 1)
+            mx_xin(p + 1)
+        op_v1(5)
+        op_v2(5)
+        op_bt(3)
+        op_c(6)
+        op_d(6)
+        op_a(6)
+        op_h(3)
+        mx_pre(7)
+        mx_rec(7)
+        mx_xin(7)
+        op_bt(4)
+        op_v1(6)
+        op_v2(6)
+        op_c(7)
+        op_d(7)
+        op_a(7)
+        op_h(4)
+        op_bt(5)
+        op_v12_half(7, 0)
+        op_bt(6)
+        op_v12_half(7, 1)
+        op_bt(7)
+        op_h(5)
+        op_h(6)
+        op_h(7)

@@ -23,7 +23,7 @@ HEAD = ["kT", "k1a", "cV", "cV", "k1b", "q", "cS", "cV", "k2", "cS", "cV", "q", 
 CAP = 15
 AHEAD = 5
 AHEAD2 = 3
-VCP = "vsvsvsvs"
+VCP = "vvvvvv"
 LOOP = "A"
 
 
@@ -46,8 +46,8 @@ def tile_ltccell_pa_kernel(tc, x, h, tau, W_in, W_rec, gate_w, gate_b, out_0, ou
         nc.sync.dma_start(out=tg[0:4, :], in_=tau.rearrange("(a c) -> a c", c=OB))
         nc.sync.dma_start(out=tg[4:8, :], in_=gate_b.rearrange("(a c) -> a c", c=OB))
 
-        x_v = x.rearrange("(i p) k -> p i k", p=P)
-        h_v = h.rearrange("(i p) k -> p i k", p=P)
+        x_v = x.rearrange("(p i) k -> p i k", p=P)
+        h_v = h.rearrange("(p i) k -> p i k", p=P)
         x_sb, h_sb = [], []
         for bp in range(2):
             xt = keep.tile([P, 2 * IN], BF16, name="x_sb%d" % bp)
@@ -199,8 +199,8 @@ def tile_ltccell_pa_kernel(tc, x, h, tau, W_in, W_rec, gate_w, gate_b, out_0, ou
             dm = keep.tile([P, 1], F32, name="dm")
             nc.scalar.activation(out=dm[:], in_=small["ln"][:, 0:1], func=ACT.Sigmoid)
 
-        o0_v = out_0.rearrange("(i p) o -> p i o", p=P)
-        o1_v = out_1.rearrange("(i p) o -> p i o", p=P)
+        o0_v = out_0.rearrange("(p i) o -> p i o", p=P)
+        o1_v = out_1.rearrange("(p i) o -> p i o", p=P)
         R = {}
         K = {}
 

@@ -23,7 +23,7 @@ HEAD = ["kT", "k1a", "cV", "cV", "k1b", "q", "cS", "cV", "k2", "cS", "cV", "q", 
 CAP = 15
 AHEAD = 5
 AHEAD2 = 3
-VCP = "vvvvvv"
+VCP = "vsvsvsvs"
 LOOP = "A"
 
 
@@ -43,16 +43,16 @@ def tile_ltccell_pa_kernel(tc, x, h, tau, W_in, W_rec, gate_w, gate_b, out_0, ou
 
         tg = keep.tile([P, 2 * P], BF16, name="tg")
         nc.vector.memset(tg[:], 0.0)
-        nc.sync.dma_start(out=tg[0:4, :], in_=tau.rearrange("(a c) -> a c", c=OB))
-        nc.sync.dma_start(out=tg[4:8, :], in_=gate_b.rearrange("(a c) -> a c", c=OB))
 
-        x_v = x.rearrange("(p i) k -> p i k", p=P)
-        h_v = h.rearrange("(p i) k -> p i k", p=P)
+        x_v = x.rearrange("(i p) k -> p i k", p=P)
+        h_v = h.rearrange("(i p) k -> p i k", p=P)
         x_sb, h_sb = [], []
         for bp in range(2):
             xt = keep.tile([P, 2 * IN], BF16, name="x_sb%d" % bp)
             nc.sync.dma_start(out=xt[:].rearrange("p (i k) -> p i k", i=2), in_=x_v[:, 2 * bp:2 * bp + 2, :])
             x_sb.append(xt)
+        nc.sync.dma_start(out=tg[0:4, :], in_=tau.rearrange("(a c) -> a c", c=OB))
+        nc.sync.dma_start(out=tg[4:8, :], in_=gate_b.rearrange("(a c) -> a c", c=OB))
         for bp in range(2):
             ht = keep.tile([P, 2 * H], BF16, name="h_sb%d" % bp)
             nc.sync.dma_start(out=ht[:].rearrange("p (i k) -> p i k", i=2), in_=h_v[:, 2 * bp:2 * bp + 2, :])
@@ -199,8 +199,8 @@ def tile_ltccell_pa_kernel(tc, x, h, tau, W_in, W_rec, gate_w, gate_b, out_0, ou
             dm = keep.tile([P, 1], F32, name="dm")
             nc.scalar.activation(out=dm[:], in_=small["ln"][:, 0:1], func=ACT.Sigmoid)
 
-        o0_v = out_0.rearrange("(p i) o -> p i o", p=P)
-        o1_v = out_1.rearrange("(p i) o -> p i o", p=P)
+        o0_v = out_0.rearrange("(i p) o -> p i o", p=P)
+        o1_v = out_1.rearrange("(i p) o -> p i o", p=P)
         R = {}
         K = {}
 

from contextlib import ExitStack

import concourse.mybir as mybir
from concourse.masks import make_identity

F32 = mybir.dt.float32
BF16 = mybir.dt.bfloat16
U32 = mybir.dt.uint32
U8 = mybir.dt.uint8
FP8X4 = mybir.dt.float8_e4m3fn_x4
ACT = mybir.ActivationFunctionType
ALU = mybir.AluOpType

P = 128
B, IN, H = 512, 512, 1024
OB = 256
NBLK = H // OB
NROUND = 2 * NBLK
FLOPS = 2 * B * H * (IN + IN + H + H)

PIN = True
HEAD = ["kT", "k1a", "cV", "cV", "k1b", "q", "cS", "cV", "k2", "cS", "cV", "q", "sig", "cV", "cS", "cV", "q", "cS", "q", "M0p", "cS", "cV", "q", "M0r", "M0x", "cS", "cS", "q", "cS", "C0"]
CAP = 15
AHEAD = 5
AHEAD2 = 3
VCP = "vsvsvsvs"
LOOP = "A"


def tile_ltccell_pa_kernel(tc, x, h, tau, W_in, W_rec, gate_w, gate_b, out_0, out_1):
    nc = tc.nc
    with ExitStack() as ctx:
        keep = ctx.enter_context(tc.tile_pool(name="keep", bufs=1))
        stage = ctx.enter_context(tc.tile_pool(name="stage", bufs=4))
        work = ctx.enter_context(tc.tile_pool(name="work", bufs=3))
        outp = ctx.enter_context(tc.tile_pool(name="outp", bufs=4))
        ps = ctx.enter_context(tc.psum_pool(name="ps", bufs=8))
        if PIN:
            ctx.enter_context(tc.manual_schedule())

        ident = keep.tile([P, P], F32, name="ident")
        make_identity(nc, ident[:])

        tg = keep.tile([P, 2 * P], BF16, name="tg")
        nc.vector.memset(tg[:], 0.0)

        x_v = x.rearrange("(i p) k -> p i k", p=P)
        h_v = h.rearrange("(i p) k -> p i k", p=P)
        x_sb, h_sb = [], []
        for bp in range(2):
            xt = keep.tile([P, 2 * IN], BF16, name="x_sb%d" % bp)
            nc.sync.dma_start(out=xt[:].rearrange("p (i k) -> p i k", i=2), in_=x_v[:, 2 * bp:2 * bp + 2, :])
            x_sb.append(xt)
        nc.sync.dma_start(out=tg[0:4, :], in_=tau.rearrange("(a c) -> a c", c=OB))
        nc.sync.dma_start(out=tg[4:8, :], in_=gate_b.rearrange("(a c) -> a c", c=OB))
        for bp in range(2):
            ht = keep.tile([P, 2 * H], BF16, name="h_sb%d" % bp)
            nc.sync.dma_start(out=ht[:].rearrange("p (i k) -> p i k", i=2), in_=h_v[:, 2 * bp:2 * bp + 2, :])
            h_sb.append(ht)

        gw_sb, wr_sb, wi_sb = [], [], []
        for a in range(NBLK):
            rows = slice(a * OB, (a + 1) * OB)
            gt = keep.tile([P, 2 * (IN + H)], BF16, name="gw_sb%d" % a)
            nc.sync.dma_start(out=gt[:], in_=gate_w[rows, :].rearrange("(p e) k -> p (e k)", e=2))
            it = keep.tile([P, 2 * IN], BF16, name="wi_sb%d" % a)
            nc.sync.dma_start(out=it[:], in_=W_in[rows, :].rearrange("(p e) k -> p (e k)", e=2))
            rt = keep.tile([P, 2 * H], BF16, name="wr_sb%d" % a)
            nc.sync.dma_start(out=rt[:], in_=W_rec[rows, :].rearrange("(p e) k -> p (e k)", e=2))
            gw_sb.append(gt)
            wr_sb.append(rt)
            wi_sb.append(it)

        xq = keep.tile([P, 512], U32, name="xq", align_bytes=64)
        xs = keep.tile([P, 512], U8, name="xs", align_bytes=64)
        hq = keep.tile([P, 1024], U32, name="hq", align_bytes=64)
        hs = keep.tile([P, 1024], U8, name="hs", align_bytes=64)
        hg = []
        for g in range(2):
            hgt = keep.tile([P, 2048], BF16, name="hg%d" % g, align_bytes=64)
            hg.append(hgt)
        wq, ws = [], []
        for a in range(NBLK):
            cq = keep.tile([P, 6 * OB], U32, name="wq%d" % a, align_bytes=64)
            cs = keep.tile([P, 6 * OB], U8, name="ws%d" % a, align_bytes=64)
            wq.append(cq)
            ws.append(cs)

        stream = [(x_sb[0], IN // 2, 0, "x", 0, []), (x_sb[1], IN // 2, 0, "x", 1, ["x"]),
                  (h_sb[0], H // 2, 0, "h0", 0, []), (h_sb[0], H // 2, 256, "h1", 0, []),
                  (h_sb[1], H // 2, 0, "h0", 1, ["h0"]), (h_sb[1], H // 2, 256, "h1", 1, ["h1"])]
        dest = {"x": (xq[:], xs[:]), "h0": (hq[:, 0:512], hs[:, 0:512]), "h1": (hq[:, 512:1024], hs[:, 512:1024])}
        gwords = (IN + H) // 2
        narrow = []
        for a in range(NBLK):
            srcs = [(gw_sb[a], gwords, 0), (gw_sb[a], gwords, 256), (gw_sb[a], gwords, 512),
                    (wi_sb[a], IN // 2, 0), (wr_sb[a], H // 2, 0), (wr_sb[a], H // 2, 256)]
            for m in range(6):
                if a == 0 and m // 2 == 1:
                    key = "w0_1_%d" % (m % 2)
                    stream.append((srcs[m][0], srcs[m][1], srcs[m][2], key, 0, [key]))
                    dest[key] = (wq[a][:, m * OB:(m + 1) * OB], ws[a][:, m * OB:(m + 1) * OB])
                    narrow.append(key)
                else:
                    key = "w%d_%d" % (a, m // 2)
                    stream.append((srcs[m][0], srcs[m][1], srcs[m][2], key, m % 2, [key] if m % 2 == 1 else []))
                    dest[key] = (wq[a][:, (m // 2) * 512:(m // 2 + 1) * 512], ws[a][:, (m // 2) * 512:(m // 2 + 1) * 512])

        st = {"ti": 0, "ci": 0, "qi": 0, "cap": CAP, "ahead": AHEAD}
        banks = {}
        groups = {"h0": hg[0], "h1": hg[1]}
        ready = []

        def tp():
            n = st["ti"]
            st["ti"] = n + 1
            src, row_words, first = stream[n][0:3]
            s32 = src[:].bitcast(F32)
            bank = ps.tile([P, 512], F32, name="bank")
            for e in range(2):
                for u in range(2):
                    c0 = e * row_words + first + u * P
                    nc.tensor.transpose(bank[:, u * OB + e * P:u * OB + (e + 1) * P], s32[:, c0:c0 + P], ident[:])
            banks[n] = bank

        def fill():
            while st["ti"] - st["ci"] < st["ahead"] and st["ti"] < min(len(stream), st["cap"]):
                tp()

        def cp(eng):
            n = st["ci"]
            if n >= len(stream):
                return
            if st["ti"] <= n:
                tp()
            st["ci"] = n + 1
            key, half, done = stream[n][3:6]
            if key not in groups:
                grouped = stage.tile([P, 2048], BF16, name="grouped", align_bytes=64)
                groups[key] = grouped
            g32 = groups[key][:].bitcast(F32)
            dst = g32[:, half * 512:(half + 1) * 512].rearrange("p (r u) -> p r u", u=2)
            src = banks[n][:].rearrange("p (u r) -> p r u", u=2)
            if eng == "v":
                nc.vector.tensor_copy(out=dst, in_=src)
            else:
                nc.scalar.copy(out=dst, in_=src)
            ready.extend(done)

        def q():
            while st["qi"] < len(ready):
                key = ready[st["qi"]]
                st["qi"] = st["qi"] + 1
                width = 1024 if key in narrow else 2048
                nc.vector.quantize_mx(out=dest[key][0].bitcast(FP8X4), scales=dest[key][1], in_=groups[key][:, 0:width])

        small = {}

        def chain_t():
            bank = ps.tile([P, 512], F32, name="bank")
            nc.tensor.transpose(bank[:, 0:P], tg[:].bitcast(F32), ident[:])
            small["bank"] = bank

        def chain_1a():
            tb = keep.tile([P, 8], F32, name="tb")
            nc.vector.tensor_copy(out=tb[:], in_=small["bank"][:, 0:8])
            tbv = tb[:].bitcast(BF16)
            ab = keep.tile([P, 8], F32, name="ab")
            nc.scalar.activation(out=ab[:], in_=tbv[:, 0:8], func=ACT.Abs)
            ex = keep.tile([P, 8], F32, name="ex")
            nc.scalar.activation(out=ex[:], in_=ab[:], func=ACT.Exp, scale=-1.0)
            small["tbv"] = tbv
            small["ex"] = ex

        def chain_1b():
            e1 = keep.tile([P, 8], F32, name="e1")
            nc.vector.tensor_scalar_add(out=e1[:], in0=small["ex"][:], scalar1=1.0)
            rl = keep.tile([P, 8], F32, name="rl")
            nc.vector.tensor_scalar_max(out=rl[:], in0=small["tbv"][:, 0:8], scalar1=0.0)
            gbf = keep.tile([P, 8], F32, name="gbf")
            nc.vector.tensor_copy(out=gbf[:], in_=small["tbv"][:, 8:16])
            ln = keep.tile([P, 8], F32, name="ln")
            nc.scalar.activation(out=ln[:], in_=e1[:], func=ACT.Ln)
            small["rl"] = rl
            small["gbf"] = gbf
            small["ln"] = ln

        def chain_2():
            tp_ = keep.tile([P, 8], F32, name="tp_")
            nc.vector.scalar_tensor_tensor(out=tp_[:], in0=small["ln"][:], scalar=1.0, in1=small["rl"][:],
                                           op0=ALU.add, op1=ALU.add)
            rc = keep.tile([P, 8], F32, name="rc")
            nc.vector.reciprocal(out=rc[:], in_=tp_[:])
            nrc = keep.tile([P, 8], F32, name="nrc")
            nc.vector.tensor_scalar_mul(out=nrc[:], in0=rc[:], scalar1=-1.0)
            small["nrc"] = nrc

        def sig_table():
            dm = keep.tile([P, 1], F32, name="dm")
            nc.scalar.activation(out=dm[:], in_=small["ln"][:, 0:1], func=ACT.Sigmoid)

        o0_v = out_0.rearrange("(i p) o -> p i o", p=P)
        o1_v = out_1.rearrange("(i p) o -> p i o", p=P)
        R = {}
        K = {}

        def mx_pre(r):
            a, e = r // 2, r % 2
            pre = ps.tile([P, 512], F32, name="bank")
            plan = [(pre, 0, xq[:], xs[:], True, False), (pre, 1, hq[:, 0:512], hs[:, 0:512], False, False),
                    (pre, 2, hq[:, 512:1024], hs[:, 512:1024], False, True)]
            for o, qq, rc_, rs_, start, stop in plan:
                w0 = qq * OB + e * P
                nc.tensor.matmul_mx(out=o[:], lhsT=wq[a][:, w0:w0 + P].bitcast(FP8X4), lhsT_scale=ws[a][:, w0:w0 + P],
                                    rhs=rc_.bitcast(FP8X4), rhs_scale=rs_, start=start, stop=stop)
            R[r] = {"pre": pre}

        def mx_rec(r):
            a, e = r // 2, r % 2
            rec = ps.tile([P, 512], F32, name="bank")
            plan = [(rec, 4, hq[:, 0:512], hs[:, 0:512], True, False), (rec, 5, hq[:, 512:1024], hs[:, 512:1024], False, True)]
            for o, qq, rc_, rs_, start, stop in plan:
                w0 = qq * OB + e * P
                nc.tensor.matmul_mx(out=o[:], lhsT=wq[a][:, w0:w0 + P].bitcast(FP8X4), lhsT_scale=ws[a][:, w0:w0 + P],
                                    rhs=rc_.bitcast(FP8X4), rhs_scale=rs_, start=start, stop=stop)
            R[r]["rec"] = rec

        def mx_xin(k):
            a, bp = k // 2, k % 2
            xin = ps.tile([P, 512], F32, name="bank")
            for s in range(2):
                b0 = (2 * bp + s) * P
                nc.tensor.matmul_mx(out=xin[:, s * OB:(s + 1) * OB],
                                    lhsT=xq[:, b0:b0 + P].bitcast(FP8X4), lhsT_scale=xs[:, b0:b0 + P],
                                    rhs=wq[a][:, 3 * OB:4 * OB].bitcast(FP8X4), rhs_scale=ws[a][:, 3 * OB:4 * OB],
                                    start=True, stop=True)
            K[k] = {"xin": xin}

        def natural(ap):
            return ap.rearrange("q (s p e) -> q s p e", s=2, e=2)

        def by_parity(ap):
            return ap.rearrange("q (s e p) -> q s p e", s=2, e=2)

        def op_c(r):
            t1 = work.tile([P, 512], F32, name="t1")
            nc.scalar.activation(out=t1[:], in_=R[r]["pre"][:], func=ACT.Tanh, bias=small["gbf"][:, r:r + 1])
            R[r]["t1"] = t1

        def op_d(r):
            gt_ = work.tile([P, 512], F32, name="gt_")
            nc.scalar.activation(out=gt_[:], in_=R[r]["t1"][:], func=ACT.Sigmoid)
            R[r]["gt"] = gt_

        def op_v1(r):
            w = work.tile([P, 512], F32, name="w")
            nc.vector.tensor_tensor(out=w[:], in0=R[r]["gt"][:], in1=R[r]["rec"][:], op=ALU.mult)
            R[r]["w"] = w

        def op_v2(r):
            a, e = r // 2, r % 2
            hT = hg[a // 2][:].rearrange("p (b t) -> p b t", t=4)[:, :, 2 * (a % 2) + e]
            w2 = outp.tile([P, 512], F32, name="w2")
            nc.vector.scalar_tensor_tensor(out=w2[:], in0=hT, scalar=small["nrc"][:, r:r + 1], in1=R[r]["w"][:],
                                           op0=ALU.mult, op1=ALU.add)
            R[r]["w2"] = w2

        def op_v12_half(r, half):
            a, e = r // 2, r % 2
            cols = slice(half * OB, (half + 1) * OB)
            if half == 0:
                w = work.tile([P, 512], F32, name="w")
                w2 = outp.tile([P, 512], F32, name="w2")
                R[r]["w"] = w
                R[r]["w2"] = w2
            hT = hg[a // 2][:].rearrange("p (b t) -> p b t", t=4)[:, cols, 2 * (a % 2) + e]
            nc.vector.tensor_tensor(out=R[r]["w"][:, cols], in0=R[r]["gt"][:, cols], in1=R[r]["rec"][:, cols], op=ALU.mult)
            nc.vector.scalar_tensor_tensor(out=R[r]["w2"][:, cols], in0=hT, scalar=small["nrc"][:, r:r + 1],
                                           in1=R[r]["w"][:, cols], op0=ALU.mult, op1=ALU.add)

        def op_bt(k):
            a, bp = k // 2, k % 2
            wb = ps.tile([P, 512], F32, name="bank")
            for s in range(2):
                for e in range(2):
                    b0 = (2 * bp + s) * P
                    c0 = (2 * s + e) * P
                    nc.tensor.transpose(wb[:, c0:c0 + P], R[2 * a + e]["w2"][:, b0:b0 + P], ident[:])
            K[k]["wb"] = wb

        def op_a(k):
            a, bp = k // 2, k % 2
            xin_sb = outp.tile([P, 512], F32, name="xin_sb")
            nc.scalar.copy(out=natural(xin_sb[:]), in_=by_parity(K[k]["xin"][:]))
            nc.sync.dma_start(out=o0_v[:, 2 * bp:2 * bp + 2, a * OB:(a + 1) * OB],
                              in_=xin_sb[:].rearrange("q (s n) -> q s n", s=2))
            K[k]["xin_sb"] = xin_sb

        def op_h(k):
            a, bp = k // 2, k % 2
            k1 = outp.tile([P, 512], F32, name="k1")
            nc.vector.tensor_tensor(out=natural(k1[:]), in0=by_parity(K[k]["wb"][:]), in1=natural(K[k]["xin_sb"][:]),
                                    op=ALU.add)
            nc.sync.dma_start(out=o1_v[:, 2 * bp:2 * bp + 2, a * OB:(a + 1) * OB],
                              in_=k1[:].rearrange("q (s n) -> q s n", s=2))

        for t in HEAD:
            if t == "kT":
                chain_t()
            elif t == "k1a":
                chain_1a()
            elif t == "k1b":
                chain_1b()
            elif t == "k2":
                chain_2()
            elif t == "sig":
                sig_table()
            elif t == "cV":
                fill()
                cp("v")
                fill()
            elif t == "cS":
                fill()
                cp("s")
                fill()
            elif t == "q":
                q()
            elif t == "M0p":
                mx_pre(0)
            elif t == "M0r":
                mx_rec(0)
            elif t == "M0x":
                mx_xin(0)
                st["cap"] = len(stream)
                st["ahead"] = AHEAD2
            elif t == "C0":
                op_c(0)
                op_d(0)
        op_a(0)

        for p in range(6):
            q()
            if p >= 1:
                op_v1(p - 1)
                op_v2(p - 1)
            if p >= 3:
                op_bt(p - 3)
            cp("s")
            cp("s")
            if p > 0:
                op_c(p)
                op_d(p)
                op_a(p)
            cp(VCP[p])
            q()
            if p >= 3:
                op_h(p - 3)
            fill()
            mx_pre(p + 1)
            mx_rec(p + 1)
            mx_xin(p + 1)
        op_v1(5)
        op_v2(5)
        op_bt(3)
        op_c(6)
        op_d(6)
        op_a(6)
        op_h(3)
        mx_pre(7)
        mx_rec(7)
        mx_xin(7)
        op_bt(4)
        op_v1(6)
        op_v2(6)
        op_c(7)
        op_d(7)
        op_a(7)
        op_h(4)
        op_bt(5)
        op_v12_half(7, 0)
        op_bt(6)
        op_v12_half(7, 1)
        op_bt(7)
        op_h(5)
        op_h(6)
        op_h(7)
